import numpy as np
import ml_dtypes


def mxq(x, axis, fmt="e4m3"):
    dtype, down = {"e4m3": (ml_dtypes.float8_e4m3fn, 7), "e5m2": (ml_dtypes.float8_e5m2, 14)}[fmt]
    v = np.moveaxis(np.asarray(x, np.float32).astype(ml_dtypes.bfloat16).astype(np.float64), axis, -1)
    blocks = v.reshape(v.shape[:-1] + (-1, 32))
    amax = np.abs(blocks).max(-1, keepdims=True)
    byte = np.maximum(np.where(amax > 0, np.frexp(amax)[1] - 1 + 127, 0) - down, 1)
    scale = np.exp2(byte - 127.0)
    codes = (blocks / scale).astype(np.float32).astype(dtype).astype(np.float64)
    return np.moveaxis((codes * scale).reshape(v.shape), -1, axis)


WIDE = False


def mx_kscale(k):
    if not WIDE:
        return np.ones(k)
    levels = np.array([10, -10, 5, -5, 0])
    if k % 512:
        return np.exp2(np.random.permutation(np.resize(levels, k // 32))).repeat(32)
    a = np.empty((k // 512, 16))
    for p in range(k // 512):
        a[p, :8] = np.random.permutation(np.resize(levels, 8))
        for g in range(8):
            far = levels[np.abs(levels - a[p, g]) >= 10]
            a[p, g + 8] = far[np.random.randint(len(far))]
    return np.exp2(a.ravel()).repeat(32)


BF16 = ml_dtypes.bfloat16


def bf(x):
    return np.asarray(x, np.float32).astype(BF16)


def f64(x):
    return np.asarray(x).astype(np.float64)


B, S, H, HO, E = 4, 1024, 1024, 128, 8


def kahan_sum_last(x):
    s = np.zeros_like(x[..., 0])
    c = np.zeros_like(s)
    for i in range(x.shape[-1]):
        y = x[..., i] - c
        t = s + y
        c = (t - s) - y
        s = t
    return s


def setup_inputs():
    s = mx_kscale(H)
    return {"hidden_states": bf(np.random.standard_normal((B, S, H)) * s),
            "op_logits": bf(np.random.standard_normal((B, S, E)) * 1.3),
            "We": bf(np.random.standard_normal((E, H, HO)) / np.sqrt(H) / s[None, :, None]),
            "be": bf(np.random.standard_normal((E, HO)) * 0.3)}


def reference(hidden_states, op_logits, We, be):
    l = f64(op_logits)
    ex = np.exp(l - l.max(-1, keepdims=True))
    op_w = ex / ex.sum(-1, keepdims=True)
    prod = mxq(f64(hidden_states), 2, "e4m3")[:, None] @ mxq(f64(We), 1, "e4m3")[None]
    expert_out = prod.transpose(0, 2, 1, 3) + f64(be)
    weighted = expert_out * op_w[:, :, :, None]
    return kahan_sum_last(np.moveaxis(weighted, 2, -1))

@@ -1,0 +1,260 @@
+from contextlib import ExitStack
+
+import concourse.mybir as mybir
+from concourse.masks import make_identity
+
+F32 = mybir.dt.float32
+BF16 = mybir.dt.bfloat16
+U32 = mybir.dt.uint32
+U8 = mybir.dt.uint8
+FP8X4 = mybir.dt.float8_e4m3fn_x4
+ALU = mybir.AluOpType
+ACT = mybir.ActivationFunctionType
+AXIS = mybir.AxisListType
+
+P = 128
+TOKENS = 4 * 1024
+K = 1024
+EXPERTS = 8
+HO = 128
+PACK = 4
+PASSES = K // (P * PACK)
+WORD_BLOCKS = K // 2 // P
+TILES = TOKENS // P
+BANK_F32 = 512
+GROUP_EXPERTS = 2
+GROUPS = EXPERTS // GROUP_EXPERTS
+N_GROUP = GROUP_EXPERTS * HO
+BANK_TILES = BANK_F32 // N_GROUP
+PAIR = 2
+PAIRS = TILES // PAIR
+ROUND_TILES = 4
+PAIRS_PER_ROUND = ROUND_TILES // PAIR
+ROUNDS = TILES // ROUND_TILES
+SPLIT = 2
+BIAS_ROWS = SPLIT * EXPERTS
+BIAS_BLOCK = P // BIAS_ROWS
+BIAS_TILES = BANK_F32 // HO
+assert BIAS_TILES == ROUND_TILES
+
+FLOPS = 2 * TOKENS * K * EXPERTS * HO
+
+
+def tile_enhancedmathematicalreasoning_pa_t_kernel(tc, hidden_states, op_logits, We, be, out):
+    nc = tc.nc
+    x_dram = hidden_states.flatten_outer_dims().rearrange("(p j) k -> p j k", j=TILES)
+    logit_dram = op_logits.flatten_outer_dims().rearrange("(p j) e -> p j e", j=TILES)
+    out_dram = out.flatten_outer_dims().rearrange("(p j) o -> p j o", j=TILES)
+
+    with ExitStack() as stack:
+        keep = stack.enter_context(tc.tile_pool(name="keep", bufs=1))
+        stage = stack.enter_context(tc.tile_pool(name="stage", bufs=2 * PAIRS_PER_ROUND))
+        banks = stack.enter_context(tc.psum_pool(name="banks", bufs=8))
+        stack.enter_context(tc.manual_schedule())
+
+        ident_bf = keep.tile([P, P], BF16)
+        make_identity(nc, ident_bf[:])
+        ident_f32 = keep.tile([P, P], F32)
+        make_identity(nc, ident_f32[:])
+
+        logit_bf = keep.tile([P, TILES, EXPERTS], BF16)
+        nc.sync.dma_start(out=logit_bf[:], in_=logit_dram)
+        be_rows = keep.tile([P, HO], BF16)
+        nc.vector.memset(be_rows[:], 0.0)
+        nc.sync.dma_start(out=be_rows[0:EXPERTS, :], in_=be)
+
+        w_raw = keep.tile([P, GROUPS, PASSES, GROUP_EXPERTS, PACK, HO], BF16)
+
+        def load_weights(g):
+            for c in range(PASSES):
+                first_row = c * PACK * P
+                nc.sync.dma_start(
+                    out=w_raw[:, g, c, :, :, :],
+                    in_=We[
+                        g * GROUP_EXPERTS : (g + 1) * GROUP_EXPERTS, first_row : first_row + PACK * P, :
+                    ].rearrange("e (p v) o -> p e v o", v=PACK),
+                )
+
+        x_all = keep.tile([P, TILES, K], BF16)
+
+        def load_pair(a):
+            tiles = slice(a * PAIR, (a + 1) * PAIR)
+            nc.sync.dma_start(out=x_all[:, tiles, :], in_=x_dram[:, tiles, :])
+
+        load_weights(0)
+        for a in range(PAIRS // 2):
+            load_pair(a)
+        load_weights(1)
+        for a in range(PAIRS // 2, PAIRS):
+            load_pair(a)
+        for g in range(2, GROUPS):
+            load_weights(g)
+
+        repeat = keep.tile([P, P // EXPERTS, EXPERTS], BF16)
+        nc.vector.tensor_copy(
+            out=repeat[:], in_=ident_bf[:, 0:EXPERTS].unsqueeze(1).to_broadcast([P, P // EXPERTS, EXPERTS])
+        )
+        be_bank = banks.tile([P, HO], F32, tag="bank")
+        nc.tensor.matmul(
+            out=be_bank[:], lhsT=repeat[:].rearrange("p r e -> p (r e)"), rhs=be_rows[:], start=True, stop=True
+        )
+        own_tile = keep.tile([P, BIAS_BLOCK], F32)
+        nc.vector.tensor_reduce(
+            out=own_tile[:], in_=ident_f32[:].rearrange("p (j r) -> p j r", r=BIAS_ROWS), axis=AXIS.X, op=ALU.add
+        )
+        be_diag = keep.tile([P, BIAS_BLOCK, HO], BF16)
+
+        top = keep.tile([P, TILES], F32)
+        nc.vector.tensor_reduce(out=top[:], in_=logit_bf[:], axis=AXIS.X, op=ALU.max)
+        shifted = keep.tile([P, TILES, EXPERTS], F32)
+        nc.vector.tensor_tensor(
+            out=shifted[:],
+            in0=logit_bf[:],
+            in1=top[:].unsqueeze(2).to_broadcast([P, TILES, EXPERTS]),
+            op=ALU.subtract,
+        )
+        grown = keep.tile([P, TILES, EXPERTS], F32)
+        nc.scalar.activation(out=grown[:], in_=shifted[:], func=ACT.Exp)
+        for j in range(BIAS_BLOCK):
+            nc.scalar.activation(out=be_diag[:, j, :], in_=be_bank[:], func=ACT.Copy, scale=own_tile[:, j : j + 1])
+        total = keep.tile([P, TILES], F32)
+        nc.vector.tensor_reduce(out=total[:], in_=grown[:], axis=AXIS.X, op=ALU.add)
+        inverse = keep.tile([P, TILES], F32)
+        nc.vector.reciprocal(out=inverse[:], in_=total[:])
+        op_w = keep.tile([P, TILES, EXPERTS], F32)
+        nc.vector.tensor_tensor(
+            out=op_w[:],
+            in0=grown[:],
+            in1=inverse[:].unsqueeze(2).to_broadcast([P, TILES, EXPERTS]),
+            op=ALU.mult,
+        )
+
+        w_split = keep.tile([P, TILES, SPLIT, EXPERTS], BF16)
+        nc.vector.tensor_copy(out=w_split[:, :, 0, :], in_=op_w[:])
+        nc.vector.tensor_tensor(out=w_split[:, :, 1, :], in0=op_w[:], in1=w_split[:, :, 0, :], op=ALU.subtract)
+        w_rows_bank = banks.tile([P, TILES // BIAS_BLOCK, P], BF16, tag="bank")
+        for g in range(TILES // BIAS_BLOCK):
+            nc.tensor.transpose(
+                w_rows_bank[:, g, :],
+                w_split[:, g * BIAS_BLOCK : (g + 1) * BIAS_BLOCK, :, :].rearrange("p j s e -> p (j s e)"),
+                ident_bf[:],
+            )
+        w_rows = keep.tile([P, TILES // BIAS_BLOCK, P], BF16)
+        nc.scalar.copy(out=w_rows[:], in_=w_rows_bank[:])
+
+        acc = keep.tile([P, TILES, HO], F32)
+
+        def bias_terms(q):
+            first = q * BIAS_TILES
+            in_block = first % BIAS_BLOCK
+            bias_bank = banks.tile([P, BIAS_TILES, HO], F32, tag="bank")
+            nc.tensor.matmul(
+                out=bias_bank[:].rearrange("p j o -> p (j o)"),
+                lhsT=w_rows[:, first // BIAS_BLOCK, :],
+                rhs=be_diag[:, in_block : in_block + BIAS_TILES, :].rearrange("p j o -> p (j o)"),
+                start=True,
+                stop=True,
+            )
+            nc.scalar.copy(out=acc[:, first : first + BIAS_TILES, :], in_=bias_bank[:])
+
+        w_grouped = keep.tile([P, GROUPS, PASSES, N_GROUP, PACK], BF16, align_bytes=64)
+        w_codes = keep.tile([P, GROUPS, PASSES, N_GROUP], U32, align_bytes=64)
+        w_scales = keep.tile([P, GROUPS, PASSES, N_GROUP], U8, align_bytes=64)
+
+        def regroup_weights(copy, g):
+            copy(
+                out=w_grouped[:, g, :, :, :].rearrange("p c (e o) v -> p (c e) o v", e=GROUP_EXPERTS),
+                in_=w_raw[:, g, :, :, :, :].rearrange("p c e v o -> p (c e) o v"),
+            )
+
+        def quantise_weights(g):
+            nc.vector.quantize_mx(
+                out=w_codes[:, g, :, :].rearrange("p c n -> p (c n)").bitcast(FP8X4),
+                scales=w_scales[:, g, :, :].rearrange("p c n -> p (c n)"),
+                in_=w_grouped[:, g, :, :, :].rearrange("p c n v -> p (c n v)"),
+            )
+
+        regroup_weights(nc.vector.tensor_copy, 0)
+        quantise_weights(0)
+
+        x_codes = keep.tile([P, TILES, PASSES, P], U32, align_bytes=64)
+        x_scales = keep.tile([P, TILES, PASSES, P], U8, align_bytes=64)
+        x_grouped = {}
+
+        def flip_pair(a):
+            x_grouped[a] = stage.tile([P, PAIR, PASSES, P, PACK], BF16, align_bytes=64, name="x_grouped")
+            for jj in range(PAIR):
+                x_words = x_all[:, a * PAIR + jj, :].bitcast(F32)
+                flipped = banks.tile([P, WORD_BLOCKS, P], F32, tag="bank")
+                for c in range(PASSES):
+                    for u in range(2):
+                        nc.tensor.transpose(
+                            flipped[:, 2 * c + u, :], x_words[:, 2 * c * P + u : 2 * (c + 1) * P : 2], ident_f32[:]
+                        )
+                nc.scalar.copy(
+                    out=x_grouped[a][:, jj, :, :, :].bitcast(F32),
+                    in_=flipped[:].rearrange("p (c u) t -> p c t u", u=2),
+                )
+
+        def quantise_pair(a):
+            tiles = slice(a * PAIR, (a + 1) * PAIR)
+            nc.vector.quantize_mx(
+                out=x_codes[:, tiles, :, :].rearrange("p j c t -> p (j c t)").bitcast(FP8X4),
+                scales=x_scales[:, tiles, :, :].rearrange("p j c t -> p (j c t)"),
+                in_=x_grouped[a][:].rearrange("p j c t v -> p (j c t v)"),
+            )
+
+        def multiply_round(g, i):
+            products = []
+            for b in range(ROUND_TILES // BANK_TILES):
+                product = banks.tile([P, BANK_TILES, GROUP_EXPERTS, HO], F32, tag="bank")
+                for jj in range(BANK_TILES):
+                    j = i * ROUND_TILES + b * BANK_TILES + jj
+                    for c in range(PASSES):
+                        nc.tensor.matmul_mx(
+                            out=product[:, jj, :, :].rearrange("p e o -> p (e o)"),
+                            lhsT=x_codes[:, j, c, :].bitcast(FP8X4),
+                            lhsT_scale=x_scales[:, j, c, :],
+                            rhs=w_codes[:, g, c, :].bitcast(FP8X4),
+                            rhs_scale=w_scales[:, g, c, :],
+                            start=(c == 0),
+                            stop=(c == PASSES - 1),
+                        )
+                products.append(product)
+            for e in range(GROUP_EXPERTS):
+                expert = g * GROUP_EXPERTS + e
+                for n in range(ROUND_TILES):
+                    j = i * ROUND_TILES + n
+                    nc.vector.scalar_tensor_tensor(
+                        out=acc[:, j, :],
+                        in0=products[n // BANK_TILES][:, n % BANK_TILES, e, :],
+                        scalar=op_w[:, j, expert : expert + 1],
+                        in1=acc[:, j, :],
+                        op0=ALU.mult,
+                        op1=ALU.add,
+                    )
+
+        for i in range(ROUNDS + 1):
+            if i == ROUNDS // 2:
+                regroup_weights(nc.vector.tensor_copy, 1)
+            if i < ROUNDS:
+                for n in range(PAIRS_PER_ROUND):
+                    flip_pair(i * PAIRS_PER_ROUND + n)
+                bias_terms(i)
+                for n in range(PAIRS_PER_ROUND):
+                    quantise_pair(i * PAIRS_PER_ROUND + n)
+            if i == ROUNDS // 2:
+                quantise_weights(1)
+            if i > 0:
+                multiply_round(0, i - 1)
+
+        for g in range(1, GROUPS):
+            if g + 1 < GROUPS:
+                regroup_weights(nc.scalar.copy, g + 1)
+            for i in range(ROUNDS):
+                if i == ROUNDS // 2 and g + 1 < GROUPS:
+                    quantise_weights(g + 1)
+                multiply_round(g, i)
+                if g == GROUPS - 1:
+                    tiles = slice(i * ROUND_TILES, (i + 1) * ROUND_TILES)
+                    nc.sync.dma_start(out=out_dram[:, tiles, :], in_=acc[:, tiles, :])

@@ -31,6 +31,7 @@ PAIRS = TILES // PAIR
 ROUND_TILES = 4
 PAIRS_PER_ROUND = ROUND_TILES // PAIR
 ROUNDS = TILES // ROUND_TILES
+FLIP_BANKS = 4
 SPLIT = 2
 BIAS_ROWS = SPLIT * EXPERTS
 BIAS_BLOCK = P // BIAS_ROWS
@@ -48,8 +49,9 @@ def tile_enhancedmathematicalreasoning_pa_t_kernel(tc, hidden_states, op_logits,
 
     with ExitStack() as stack:
         keep = stack.enter_context(tc.tile_pool(name="keep", bufs=1))
-        stage = stack.enter_context(tc.tile_pool(name="stage", bufs=2 * PAIRS_PER_ROUND))
-        banks = stack.enter_context(tc.psum_pool(name="banks", bufs=8))
+        stage = stack.enter_context(tc.tile_pool(name="stage", bufs=8))
+        banks = stack.enter_context(tc.psum_pool(name="banks", bufs=FLIP_BANKS))
+        product_banks = stack.enter_context(tc.psum_pool(name="product_banks", bufs=8 - FLIP_BANKS))
         stack.enter_context(tc.manual_schedule())
 
         ident_bf = keep.tile([P, P], BF16)
@@ -59,9 +61,6 @@ def tile_enhancedmathematicalreasoning_pa_t_kernel(tc, hidden_states, op_logits,
 
         logit_bf = keep.tile([P, TILES, EXPERTS], BF16)
         nc.sync.dma_start(out=logit_bf[:], in_=logit_dram)
-        be_rows = keep.tile([P, HO], BF16)
-        nc.vector.memset(be_rows[:], 0.0)
-        nc.sync.dma_start(out=be_rows[0:EXPERTS, :], in_=be)
 
         w_raw = keep.tile([P, GROUPS, PASSES, GROUP_EXPERTS, PACK, HO], BF16)
 
@@ -77,33 +76,95 @@ def tile_enhancedmathematicalreasoning_pa_t_kernel(tc, hidden_states, op_logits,
 
         x_all = keep.tile([P, TILES, K], BF16)
 
-        def load_pair(a):
-            tiles = slice(a * PAIR, (a + 1) * PAIR)
+        def load_tokens(first, count):
+            tiles = slice(first, first + count)
             nc.sync.dma_start(out=x_all[:, tiles, :], in_=x_dram[:, tiles, :])
 
+        be_rows = keep.tile([P, HO], BF16)
+        nc.gpsimd.memset(be_rows[:], 0.0)
+        nc.sync.dma_start(out=be_rows[0:EXPERTS, :], in_=be)
         load_weights(0)
-        for a in range(PAIRS // 2):
-            load_pair(a)
-        load_weights(1)
-        for a in range(PAIRS // 2, PAIRS):
-            load_pair(a)
-        for g in range(2, GROUPS):
+        for j in range(ROUND_TILES):
+            load_tokens(j, 1)
+        for g in range(1, GROUPS):
             load_weights(g)
+        for a in range(PAIRS_PER_ROUND, PAIRS):
+            load_tokens(a * PAIR, PAIR)
+
+        w_grouped = keep.tile([P, GROUPS, PASSES, N_GROUP, PACK], BF16, align_bytes=64)
+        w_codes = keep.tile([P, GROUPS, PASSES, N_GROUP], U32, align_bytes=64)
+        w_scales = keep.tile([P, GROUPS, PASSES, N_GROUP], U8, align_bytes=64)
+
+        def gp(out, in_):
+            nc.gpsimd.tensor_scalar(out=out, in0=in_, scalar1=1.0, scalar2=0.0, op0=ALU.mult, op1=ALU.add)
+
+        def regroup_weights(copy, g, c):
+            copy(
+                out=w_grouped[:, g, c, :, :].rearrange("p (e o) v -> p e o v", e=GROUP_EXPERTS),
+                in_=w_raw[:, g, c, :, :, :].rearrange("p e v o -> p e o v"),
+            )
+
+        def quantise_weights(g):
+            nc.vector.quantize_mx(
+                out=w_codes[:, g, :, :].rearrange("p c n -> p (c n)").bitcast(FP8X4),
+                scales=w_scales[:, g, :, :].rearrange("p c n -> p (c n)"),
+                in_=w_grouped[:, g, :, :, :].rearrange("p c n v -> p (c n v)"),
+            )
+
+        x_codes = keep.tile([P, TILES, PASSES, P], U32, align_bytes=64)
+        x_scales = keep.tile([P, TILES, PASSES, P], U8, align_bytes=64)
+        x_grouped = {}
+        x_sorted = {}
+
+        def sort_round(i):
+            for j in range(i * ROUND_TILES, (i + 1) * ROUND_TILES):
+                x_sorted[j] = stage.tile([P, PASSES, 2, P], F32, name="x_sorted")
+                nc.scalar.copy(
+                    out=x_sorted[j][:], in_=x_all[:, j, :].bitcast(F32).rearrange("p (c q u) -> p c u q", c=PASSES, u=2)
+                )
+
+        def flip_pair(a):
+            x_grouped[a] = stage.tile([P, PAIR, PASSES, P, PACK], BF16, align_bytes=64, name="x_grouped")
+            for jj in range(PAIR):
+                j = a * PAIR + jj
+                x_words = x_all[:, j, :].bitcast(F32)
+                flipped = banks.tile([P, WORD_BLOCKS, P], F32, tag="bank")
+                for c in range(PASSES):
+                    for u in range(2):
+                        nc.tensor.transpose(
+                            flipped[:, 2 * c + u, :],
+                            x_sorted[j][:, c, u, :] if j in x_sorted else x_words[:, 2 * c * P + u : 2 * (c + 1) * P : 2],
+                            ident_f32[:],
+                        )
+                nc.scalar.copy(
+                    out=x_grouped[a][:, jj, :, :, :].bitcast(F32),
+                    in_=flipped[:].rearrange("p (c u) t -> p c t u", u=2),
+                )
+
+        def flip_round(i):
+            for n in range(PAIRS_PER_ROUND):
+                flip_pair(i * PAIRS_PER_ROUND + n)
+
+        def quantise_pair(a):
+            tiles = slice(a * PAIR, (a + 1) * PAIR)
+            nc.vector.quantize_mx(
+                out=x_codes[:, tiles, :, :].rearrange("p j c t -> p (j c t)").bitcast(FP8X4),
+                scales=x_scales[:, tiles, :, :].rearrange("p j c t -> p (j c t)"),
+                in_=x_grouped[a][:].rearrange("p j c t v -> p (j c t v)"),
+            )
+
+        def quantise_round(i):
+            for n in range(PAIRS_PER_ROUND):
+                quantise_pair(i * PAIRS_PER_ROUND + n)
 
         repeat = keep.tile([P, P // EXPERTS, EXPERTS], BF16)
         nc.vector.tensor_copy(
             out=repeat[:], in_=ident_bf[:, 0:EXPERTS].unsqueeze(1).to_broadcast([P, P // EXPERTS, EXPERTS])
         )
-        be_bank = banks.tile([P, HO], F32, tag="bank")
-        nc.tensor.matmul(
-            out=be_bank[:], lhsT=repeat[:].rearrange("p r e -> p (r e)"), rhs=be_rows[:], start=True, stop=True
-        )
         own_tile = keep.tile([P, BIAS_BLOCK], F32)
         nc.vector.tensor_reduce(
             out=own_tile[:], in_=ident_f32[:].rearrange("p (j r) -> p j r", r=BIAS_ROWS), axis=AXIS.X, op=ALU.add
         )
-        be_diag = keep.tile([P, BIAS_BLOCK, HO], BF16)
-
         top = keep.tile([P, TILES], F32)
         nc.vector.tensor_reduce(out=top[:], in_=logit_bf[:], axis=AXIS.X, op=ALU.max)
         shifted = keep.tile([P, TILES, EXPERTS], F32)
@@ -115,12 +176,25 @@ def tile_enhancedmathematicalreasoning_pa_t_kernel(tc, hidden_states, op_logits,
         )
         grown = keep.tile([P, TILES, EXPERTS], F32)
         nc.scalar.activation(out=grown[:], in_=shifted[:], func=ACT.Exp)
+        grown_split = keep.tile([P, TILES, SPLIT, EXPERTS], BF16)
+        nc.scalar.copy(out=grown_split[:, :, 0, :], in_=grown[:])
+        be_bank = banks.tile([P, HO], F32, tag="bank")
+        nc.tensor.matmul(
+            out=be_bank[:], lhsT=repeat[:].rearrange("p r e -> p (r e)"), rhs=be_rows[:], start=True, stop=True
+        )
+        be_diag = keep.tile([P, BIAS_BLOCK, HO], BF16)
         for j in range(BIAS_BLOCK):
             nc.scalar.activation(out=be_diag[:, j, :], in_=be_bank[:], func=ACT.Copy, scale=own_tile[:, j : j + 1])
+        regroup_weights(nc.vector.tensor_copy, 0, 0)
+        nc.vector.tensor_tensor(
+            out=grown_split[:, :, 1, :], in0=grown[:], in1=grown_split[:, :, 0, :], op=ALU.subtract
+        )
         total = keep.tile([P, TILES], F32)
         nc.vector.tensor_reduce(out=total[:], in_=grown[:], axis=AXIS.X, op=ALU.add)
+        regroup_weights(nc.vector.tensor_copy, 0, 1)
         inverse = keep.tile([P, TILES], F32)
         nc.vector.reciprocal(out=inverse[:], in_=total[:])
+        quantise_weights(0)
         op_w = keep.tile([P, TILES, EXPERTS], F32)
         nc.vector.tensor_tensor(
             out=op_w[:],
@@ -128,24 +202,26 @@ def tile_enhancedmathematicalreasoning_pa_t_kernel(tc, hidden_states, op_logits,
             in1=inverse[:].unsqueeze(2).to_broadcast([P, TILES, EXPERTS]),
             op=ALU.mult,
         )
-
-        w_split = keep.tile([P, TILES, SPLIT, EXPERTS], BF16)
-        nc.vector.tensor_copy(out=w_split[:, :, 0, :], in_=op_w[:])
-        nc.vector.tensor_tensor(out=w_split[:, :, 1, :], in0=op_w[:], in1=w_split[:, :, 0, :], op=ALU.subtract)
         w_rows_bank = banks.tile([P, TILES // BIAS_BLOCK, P], BF16, tag="bank")
-        for g in range(TILES // BIAS_BLOCK):
+        for q in range(TILES // BIAS_BLOCK):
             nc.tensor.transpose(
-                w_rows_bank[:, g, :],
-                w_split[:, g * BIAS_BLOCK : (g + 1) * BIAS_BLOCK, :, :].rearrange("p j s e -> p (j s e)"),
+                w_rows_bank[:, q, :],
+                grown_split[:, q * BIAS_BLOCK : (q + 1) * BIAS_BLOCK, :, :].rearrange("p j s e -> p (j s e)"),
                 ident_bf[:],
             )
         w_rows = keep.tile([P, TILES // BIAS_BLOCK, P], BF16)
         nc.scalar.copy(out=w_rows[:], in_=w_rows_bank[:])
+        flip_round(0)
+        for g in range(1, GROUPS):
+            for c in range(PASSES):
+                regroup_weights(nc.vector.tensor_copy if (g, c) == (1, 1) else gp, g, c)
+        quantise_round(0)
+        quantise_weights(1)
 
         acc = keep.tile([P, TILES, HO], F32)
 
-        def bias_terms(q):
-            first = q * BIAS_TILES
+        def bias_terms(i):
+            first = i * BIAS_TILES
             in_block = first % BIAS_BLOCK
             bias_bank = banks.tile([P, BIAS_TILES, HO], F32, tag="bank")
             nc.tensor.matmul(
@@ -155,59 +231,16 @@ def tile_enhancedmathematicalreasoning_pa_t_kernel(tc, hidden_states, op_logits,
                 start=True,
                 stop=True,
             )
-            nc.scalar.copy(out=acc[:, first : first + BIAS_TILES, :], in_=bias_bank[:])
-
-        w_grouped = keep.tile([P, GROUPS, PASSES, N_GROUP, PACK], BF16, align_bytes=64)
-        w_codes = keep.tile([P, GROUPS, PASSES, N_GROUP], U32, align_bytes=64)
-        w_scales = keep.tile([P, GROUPS, PASSES, N_GROUP], U8, align_bytes=64)
-
-        def regroup_weights(copy, g):
-            copy(
-                out=w_grouped[:, g, :, :, :].rearrange("p c (e o) v -> p (c e) o v", e=GROUP_EXPERTS),
-                in_=w_raw[:, g, :, :, :, :].rearrange("p c e v o -> p (c e) o v"),
-            )
-
-        def quantise_weights(g):
-            nc.vector.quantize_mx(
-                out=w_codes[:, g, :, :].rearrange("p c n -> p (c n)").bitcast(FP8X4),
-                scales=w_scales[:, g, :, :].rearrange("p c n -> p (c n)"),
-                in_=w_grouped[:, g, :, :, :].rearrange("p c n v -> p (c n v)"),
-            )
-
-        regroup_weights(nc.vector.tensor_copy, 0)
-        quantise_weights(0)
-
-        x_codes = keep.tile([P, TILES, PASSES, P], U32, align_bytes=64)
-        x_scales = keep.tile([P, TILES, PASSES, P], U8, align_bytes=64)
-        x_grouped = {}
-
-        def flip_pair(a):
-            x_grouped[a] = stage.tile([P, PAIR, PASSES, P, PACK], BF16, align_bytes=64, name="x_grouped")
-            for jj in range(PAIR):
-                x_words = x_all[:, a * PAIR + jj, :].bitcast(F32)
-                flipped = banks.tile([P, WORD_BLOCKS, P], F32, tag="bank")
-                for c in range(PASSES):
-                    for u in range(2):
-                        nc.tensor.transpose(
-                            flipped[:, 2 * c + u, :], x_words[:, 2 * c * P + u : 2 * (c + 1) * P : 2], ident_f32[:]
-                        )
-                nc.scalar.copy(
-                    out=x_grouped[a][:, jj, :, :, :].bitcast(F32),
-                    in_=flipped[:].rearrange("p (c u) t -> p c t u", u=2),
+            for n in range(BIAS_TILES):
+                j = first + n
+                nc.scalar.activation(
+                    out=acc[:, j, :], in_=bias_bank[:, n, :], func=ACT.Copy, scale=inverse[:, j : j + 1]
                 )
 
-        def quantise_pair(a):
-            tiles = slice(a * PAIR, (a + 1) * PAIR)
-            nc.vector.quantize_mx(
-                out=x_codes[:, tiles, :, :].rearrange("p j c t -> p (j c t)").bitcast(FP8X4),
-                scales=x_scales[:, tiles, :, :].rearrange("p j c t -> p (j c t)"),
-                in_=x_grouped[a][:].rearrange("p j c t v -> p (j c t v)"),
-            )
-
-        def multiply_round(g, i):
+        def multiply_unit(i, g):
             products = []
             for b in range(ROUND_TILES // BANK_TILES):
-                product = banks.tile([P, BANK_TILES, GROUP_EXPERTS, HO], F32, tag="bank")
+                product = product_banks.tile([P, BANK_TILES, GROUP_EXPERTS, HO], F32, tag="product")
                 for jj in range(BANK_TILES):
                     j = i * ROUND_TILES + b * BANK_TILES + jj
                     for c in range(PASSES):
@@ -234,27 +267,27 @@ def tile_enhancedmathematicalreasoning_pa_t_kernel(tc, hidden_states, op_logits,
                         op1=ALU.add,
                     )
 
-        for i in range(ROUNDS + 1):
-            if i == ROUNDS // 2:
-                regroup_weights(nc.vector.tensor_copy, 1)
-            if i < ROUNDS:
-                for n in range(PAIRS_PER_ROUND):
-                    flip_pair(i * PAIRS_PER_ROUND + n)
-                bias_terms(i)
-                for n in range(PAIRS_PER_ROUND):
-                    quantise_pair(i * PAIRS_PER_ROUND + n)
-            if i == ROUNDS // 2:
-                quantise_weights(1)
-            if i > 0:
-                multiply_round(0, i - 1)
-
-        for g in range(1, GROUPS):
-            if g + 1 < GROUPS:
-                regroup_weights(nc.scalar.copy, g + 1)
-            for i in range(ROUNDS):
-                if i == ROUNDS // 2 and g + 1 < GROUPS:
-                    quantise_weights(g + 1)
-                multiply_round(g, i)
-                if g == GROUPS - 1:
-                    tiles = slice(i * ROUND_TILES, (i + 1) * ROUND_TILES)
-                    nc.sync.dma_start(out=out_dram[:, tiles, :], in_=acc[:, tiles, :])
+        bias_terms(0)
+        for s in range(ROUNDS):
+            for g in range(GROUPS):
+                multiply_unit(s, g)
+                if s == 0:
+                    if g == 0:
+                        bias_terms(1)
+                    elif g == 1:
+                        flip_round(1)
+                        quantise_weights(2)
+                    elif g == 2:
+                        flip_round(2)
+                        quantise_weights(3)
+                        quantise_round(1)
+                        sort_round(3)
+                elif g == 1 and s + 1 < ROUNDS:
+                    bias_terms(s + 1)
+                    if s + 2 < ROUNDS:
+                        flip_round(s + 2)
+                    quantise_round(s + 1)
+                    if s + 3 < ROUNDS:
+                        sort_round(s + 3)
+            tiles = slice(s * ROUND_TILES, (s + 1) * ROUND_TILES)
+            nc.sync.dma_start(out=out_dram[:, tiles, :], in_=acc[:, tiles, :])

@@ -86,17 +86,16 @@ def tile_enhancedmathematicalreasoning_pa_t_kernel(tc, hidden_states, op_logits,
         load_weights(0)
         for j in range(ROUND_TILES):
             load_tokens(j, 1)
-        for g in range(1, GROUPS):
-            load_weights(g)
+        load_weights(1)
+        load_weights(2)
         for a in range(PAIRS_PER_ROUND, PAIRS):
             load_tokens(a * PAIR, PAIR)
+            if a == 2 * PAIRS_PER_ROUND - 1:
+                load_weights(3)
 
         w_grouped = keep.tile([P, GROUPS, PASSES, N_GROUP, PACK], BF16, align_bytes=64)
         w_codes = keep.tile([P, GROUPS, PASSES, N_GROUP], U32, align_bytes=64)
         w_scales = keep.tile([P, GROUPS, PASSES, N_GROUP], U8, align_bytes=64)
-
-        def gp(out, in_):
-            nc.gpsimd.tensor_scalar(out=out, in0=in_, scalar1=1.0, scalar2=0.0, op0=ALU.mult, op1=ALU.add)
 
         def regroup_weights(copy, g, c):
             copy(
@@ -183,8 +182,13 @@ def tile_enhancedmathematicalreasoning_pa_t_kernel(tc, hidden_states, op_logits,
             out=be_bank[:], lhsT=repeat[:].rearrange("p r e -> p (r e)"), rhs=be_rows[:], start=True, stop=True
         )
         be_diag = keep.tile([P, BIAS_BLOCK, HO], BF16)
-        for j in range(BIAS_BLOCK):
+
+        def place_be(j):
             nc.scalar.activation(out=be_diag[:, j, :], in_=be_bank[:], func=ACT.Copy, scale=own_tile[:, j : j + 1])
+
+        for j in range(BIAS_TILES):
+            place_be(j)
+        flip_pair(0)
         regroup_weights(nc.vector.tensor_copy, 0, 0)
         nc.vector.tensor_tensor(
             out=grown_split[:, :, 1, :], in0=grown[:], in1=grown_split[:, :, 0, :], op=ALU.subtract
@@ -211,11 +215,11 @@ def tile_enhancedmathematicalreasoning_pa_t_kernel(tc, hidden_states, op_logits,
             )
         w_rows = keep.tile([P, TILES // BIAS_BLOCK, P], BF16)
         nc.scalar.copy(out=w_rows[:], in_=w_rows_bank[:])
-        flip_round(0)
-        for g in range(1, GROUPS):
-            for c in range(PASSES):
-                regroup_weights(nc.vector.tensor_copy if (g, c) == (1, 1) else gp, g, c)
-        quantise_round(0)
+        flip_pair(1)
+        quantise_pair(0)
+        for c in range(PASSES):
+            regroup_weights(nc.vector.tensor_copy, 1, c)
+        quantise_pair(1)
         quantise_weights(1)
 
         acc = keep.tile([P, TILES, HO], F32)
@@ -268,26 +272,34 @@ def tile_enhancedmathematicalreasoning_pa_t_kernel(tc, hidden_states, op_logits,
                     )
 
         bias_terms(0)
-        for s in range(ROUNDS):
+        for j in range(BIAS_TILES, BIAS_BLOCK):
+            place_be(j)
+        regroup_weights(nc.scalar.copy, 2, 0)
+        multiply_unit(0, 0)
+        regroup_weights(nc.vector.tensor_copy, 2, 1)
+        bias_terms(1)
+        regroup_weights(nc.scalar.copy, 3, 0)
+        multiply_unit(0, 1)
+        flip_round(1)
+        quantise_weights(2)
+        regroup_weights(nc.scalar.copy, 3, 1)
+        quantise_pair(2)
+        multiply_unit(0, 2)
+        flip_round(2)
+        quantise_pair(3)
+        quantise_weights(3)
+        multiply_unit(0, 3)
+        sort_round(3)
+        for s in range(1, ROUNDS):
             for g in range(GROUPS):
                 multiply_unit(s, g)
-                if s == 0:
-                    if g == 0:
-                        bias_terms(1)
-                    elif g == 1:
-                        flip_round(1)
-                        quantise_weights(2)
-                    elif g == 2:
-                        flip_round(2)
-                        quantise_weights(3)
-                        quantise_round(1)
-                        sort_round(3)
-                elif g == 1 and s + 1 < ROUNDS:
+                if g == 1 and s + 1 < ROUNDS:
                     bias_terms(s + 1)
                     if s + 2 < ROUNDS:
                         flip_round(s + 2)
                     quantise_round(s + 1)
                     if s + 3 < ROUNDS:
                         sort_round(s + 3)
-            tiles = slice(s * ROUND_TILES, (s + 1) * ROUND_TILES)
-            nc.sync.dma_start(out=out_dram[:, tiles, :], in_=acc[:, tiles, :])
+            for r in [0, 1] if s == 1 else [s]:
+                tiles = slice(r * ROUND_TILES, (r + 1) * ROUND_TILES)
+                nc.sync.dma_start(out=out_dram[:, tiles, :], in_=acc[:, tiles, :])

@@ -278,28 +278,26 @@ def tile_enhancedmathematicalreasoning_pa_t_kernel(tc, hidden_states, op_logits,
         multiply_unit(0, 0)
         regroup_weights(nc.vector.tensor_copy, 2, 1)
         bias_terms(1)
-        regroup_weights(nc.scalar.copy, 3, 0)
-        multiply_unit(0, 1)
         flip_round(1)
+        multiply_unit(0, 1)
+        regroup_weights(nc.scalar.copy, 3, 0)
         quantise_weights(2)
+        quantise_round(1)
         regroup_weights(nc.scalar.copy, 3, 1)
-        quantise_pair(2)
-        multiply_unit(0, 2)
+        bias_terms(2)
         flip_round(2)
-        quantise_pair(3)
-        quantise_weights(3)
-        multiply_unit(0, 3)
-        sort_round(3)
-        for s in range(1, ROUNDS):
-            for g in range(GROUPS):
-                multiply_unit(s, g)
-                if g == 1 and s + 1 < ROUNDS:
-                    bias_terms(s + 1)
+        for s in range(1, ROUNDS + 1):
+            units = [(s, 0), (s - 1, 2), (s, 1), (s - 1, 3)] if s < ROUNDS else [(s - 1, 2), (s - 1, 3)]
+            for n, (i, g) in enumerate(units):
+                multiply_unit(i, g)
+                if n == 0 and s == 1:
+                    quantise_weights(3)
+                if n == 1 and s + 1 < ROUNDS:
                     if s + 2 < ROUNDS:
+                        bias_terms(s + 2)
                         flip_round(s + 2)
                     quantise_round(s + 1)
                     if s + 3 < ROUNDS:
                         sort_round(s + 3)
-            for r in [0, 1] if s == 1 else [s]:
-                tiles = slice(r * ROUND_TILES, (r + 1) * ROUND_TILES)
-                nc.sync.dma_start(out=out_dram[:, tiles, :], in_=acc[:, tiles, :])
+            tiles = slice((s - 1) * ROUND_TILES, s * ROUND_TILES)
+            nc.sync.dma_start(out=out_dram[:, tiles, :], in_=acc[:, tiles, :])

@@ -115,8 +115,8 @@ def tile_enhancedmathematicalreasoning_pa_t_kernel(tc, hidden_states, op_logits,
         x_grouped = {}
         x_sorted = {}
 
-        def sort_round(i):
-            for j in range(i * ROUND_TILES, (i + 1) * ROUND_TILES):
+        def sort_pair(a):
+            for j in range(a * PAIR, (a + 1) * PAIR):
                 x_sorted[j] = stage.tile([P, PASSES, 2, P], F32, name="x_sorted")
                 nc.scalar.copy(
                     out=x_sorted[j][:], in_=x_all[:, j, :].bitcast(F32).rearrange("p (c q u) -> p c u q", c=PASSES, u=2)
@@ -139,6 +139,14 @@ def tile_enhancedmathematicalreasoning_pa_t_kernel(tc, hidden_states, op_logits,
                     out=x_grouped[a][:, jj, :, :, :].bitcast(F32),
                     in_=flipped[:].rearrange("p (c u) t -> p c t u", u=2),
                 )
+
+        def flip_next(a):
+            if a < PAIRS:
+                if a % PAIRS_PER_ROUND == 0:
+                    bias_terms(a // PAIRS_PER_ROUND)
+                flip_pair(a)
+            if a + 1 < PAIRS:
+                sort_pair(a + 1)
 
         def flip_round(i):
             for n in range(PAIRS_PER_ROUND):
@@ -278,26 +286,28 @@ def tile_enhancedmathematicalreasoning_pa_t_kernel(tc, hidden_states, op_logits,
         multiply_unit(0, 0)
         regroup_weights(nc.vector.tensor_copy, 2, 1)
         bias_terms(1)
-        flip_round(1)
+        flip_pair(2)
         multiply_unit(0, 1)
         regroup_weights(nc.scalar.copy, 3, 0)
         quantise_weights(2)
-        quantise_round(1)
+        flip_pair(3)
         regroup_weights(nc.scalar.copy, 3, 1)
+        quantise_round(1)
         bias_terms(2)
-        flip_round(2)
+        flip_pair(4)
         for s in range(1, ROUNDS + 1):
             units = [(s, 0), (s - 1, 2), (s, 1), (s - 1, 3)] if s < ROUNDS else [(s - 1, 2), (s - 1, 3)]
             for n, (i, g) in enumerate(units):
                 multiply_unit(i, g)
                 if n == 0 and s == 1:
                     quantise_weights(3)
-                if n == 1 and s + 1 < ROUNDS:
-                    if s + 2 < ROUNDS:
-                        bias_terms(s + 2)
-                        flip_round(s + 2)
-                    quantise_round(s + 1)
-                    if s + 3 < ROUNDS:
-                        sort_round(s + 3)
+                if n == 0:
+                    flip_next(2 * s + 3)
+                if n == 2:
+                    flip_next(2 * s + 4)
+                if n == 0 and s + 1 < ROUNDS:
+                    quantise_pair(PAIRS_PER_ROUND * (s + 1))
+                if n == 2 and s + 1 < ROUNDS:
+                    quantise_pair(PAIRS_PER_ROUND * (s + 1) + 1)
             tiles = slice((s - 1) * ROUND_TILES, s * ROUND_TILES)
             nc.sync.dma_start(out=out_dram[:, tiles, :], in_=acc[:, tiles, :])

@@ -32,6 +32,7 @@ ROUND_TILES = 4
 PAIRS_PER_ROUND = ROUND_TILES // PAIR
 ROUNDS = TILES // ROUND_TILES
 FLIP_BANKS = 4
+RUN = 4
 SPLIT = 2
 BIAS_ROWS = SPLIT * EXPERTS
 BIAS_BLOCK = P // BIAS_ROWS
@@ -54,6 +55,15 @@ def tile_enhancedmathematicalreasoning_pa_t_kernel(tc, hidden_states, op_logits,
         product_banks = stack.enter_context(tc.psum_pool(name="product_banks", bufs=8 - FLIP_BANKS))
         stack.enter_context(tc.manual_schedule())
 
+        zeros = keep.tile([P, BANK_F32], BF16)
+        nc.vector.memset(zeros[:], 0.0)
+
+        def warm_up(count):
+            idle = product_banks.tile([P, BANK_F32], F32, tag="product")
+            for n in range(count):
+                nc.tensor.matmul(out=idle[:], lhsT=zeros[:, 0:P], rhs=zeros[:], start=True, stop=True)
+
+        warm_up(8)
         ident_bf = keep.tile([P, P], BF16)
         make_identity(nc, ident_bf[:])
         ident_f32 = keep.tile([P, P], F32)
@@ -64,8 +74,8 @@ def tile_enhancedmathematicalreasoning_pa_t_kernel(tc, hidden_states, op_logits,
 
         w_raw = keep.tile([P, GROUPS, PASSES, GROUP_EXPERTS, PACK, HO], BF16)
 
-        def load_weights(g):
-            for c in range(PASSES):
+        def load_weights(g, *passes):
+            for c in passes or range(PASSES):
                 first_row = c * PACK * P
                 nc.sync.dma_start(
                     out=w_raw[:, g, c, :, :, :],
@@ -83,8 +93,10 @@ def tile_enhancedmathematicalreasoning_pa_t_kernel(tc, hidden_states, op_logits,
         be_rows = keep.tile([P, HO], BF16)
         nc.gpsimd.memset(be_rows[:], 0.0)
         nc.sync.dma_start(out=be_rows[0:EXPERTS, :], in_=be)
-        load_weights(0)
-        for j in range(ROUND_TILES):
+        for c in range(PASSES):
+            load_tokens(c, 1)
+            load_weights(0, c)
+        for j in range(PASSES, ROUND_TILES):
             load_tokens(j, 1)
         load_weights(1)
         load_weights(2)
@@ -99,8 +111,8 @@ def tile_enhancedmathematicalreasoning_pa_t_kernel(tc, hidden_states, op_logits,
 
         def regroup_weights(copy, g, c):
             copy(
-                out=w_grouped[:, g, c, :, :].rearrange("p (e o) v -> p e o v", e=GROUP_EXPERTS),
-                in_=w_raw[:, g, c, :, :, :].rearrange("p e v o -> p e o v"),
+                out=w_grouped[:, g, c, :, :].rearrange("p (e q i) v -> p e q v i", e=GROUP_EXPERTS, i=RUN),
+                in_=w_raw[:, g, c, :, :, :].rearrange("p e v (q i) -> p e q v i", i=RUN),
             )
 
         def quantise_weights(g):
@@ -225,9 +237,9 @@ def tile_enhancedmathematicalreasoning_pa_t_kernel(tc, hidden_states, op_logits,
         nc.scalar.copy(out=w_rows[:], in_=w_rows_bank[:])
         flip_pair(1)
         quantise_pair(0)
-        for c in range(PASSES):
-            regroup_weights(nc.vector.tensor_copy, 1, c)
+        regroup_weights(nc.vector.tensor_copy, 1, 0)
         quantise_pair(1)
+        regroup_weights(nc.vector.tensor_copy, 1, 1)
         quantise_weights(1)
 
         acc = keep.tile([P, TILES, HO], F32)
@@ -249,10 +261,13 @@ def tile_enhancedmathematicalreasoning_pa_t_kernel(tc, hidden_states, op_logits,
                     out=acc[:, j, :], in_=bias_bank[:, n, :], func=ACT.Copy, scale=inverse[:, j : j + 1]
                 )
 
-        def multiply_unit(i, g):
+        def multiply_unit(i, g, spare=False):
             products = []
             for b in range(ROUND_TILES // BANK_TILES):
-                product = product_banks.tile([P, BANK_TILES, GROUP_EXPERTS, HO], F32, tag="product")
+                if spare:
+                    product = banks.tile([P, BANK_TILES, GROUP_EXPERTS, HO], F32, tag="bank")
+                else:
+                    product = product_banks.tile([P, BANK_TILES, GROUP_EXPERTS, HO], F32, tag="product")
                 for jj in range(BANK_TILES):
                     j = i * ROUND_TILES + b * BANK_TILES + jj
                     for c in range(PASSES):
@@ -298,7 +313,7 @@ def tile_enhancedmathematicalreasoning_pa_t_kernel(tc, hidden_states, op_logits,
         for s in range(1, ROUNDS + 1):
             units = [(s, 0), (s - 1, 2), (s, 1), (s - 1, 3)] if s < ROUNDS else [(s - 1, 2), (s - 1, 3)]
             for n, (i, g) in enumerate(units):
-                multiply_unit(i, g)
+                multiply_unit(i, g, spare=s >= ROUNDS - 1 and n % 2 == 0)
                 if n == 0 and s == 1:
                     quantise_weights(3)
                 if n == 0:

@@ -154,8 +154,6 @@ def tile_enhancedmathematicalreasoning_pa_t_kernel(tc, hidden_states, op_logits,
 
         def flip_next(a):
             if a < PAIRS:
-                if a % PAIRS_PER_ROUND == 0:
-                    bias_terms(a // PAIRS_PER_ROUND)
                 flip_pair(a)
             if a + 1 < PAIRS:
                 sort_pair(a + 1)
@@ -320,9 +318,12 @@ def tile_enhancedmathematicalreasoning_pa_t_kernel(tc, hidden_states, op_logits,
                     flip_next(2 * s + 3)
                 if n == 2:
                     flip_next(2 * s + 4)
+                if n == 2 and s + 2 < ROUNDS:
+                    bias_terms(s + 2)
                 if n == 0 and s + 1 < ROUNDS:
                     quantise_pair(PAIRS_PER_ROUND * (s + 1))
                 if n == 2 and s + 1 < ROUNDS:
                     quantise_pair(PAIRS_PER_ROUND * (s + 1) + 1)
-            tiles = slice((s - 1) * ROUND_TILES, s * ROUND_TILES)
-            nc.sync.dma_start(out=out_dram[:, tiles, :], in_=acc[:, tiles, :])
+            step = ROUND_TILES if s < ROUNDS else 1
+            for j in range((s - 1) * ROUND_TILES, s * ROUND_TILES, step):
+                nc.sync.dma_start(out=out_dram[:, j : j + step, :], in_=acc[:, j : j + step, :])

@@ -51,6 +51,7 @@ def tile_enhancedmathematicalreasoning_pa_t_kernel(tc, hidden_states, op_logits,
     with ExitStack() as stack:
         keep = stack.enter_context(tc.tile_pool(name="keep", bufs=1))
         stage = stack.enter_context(tc.tile_pool(name="stage", bufs=8))
+        tail = stack.enter_context(tc.tile_pool(name="tail", bufs=2))
         banks = stack.enter_context(tc.psum_pool(name="banks", bufs=FLIP_BANKS))
         product_banks = stack.enter_context(tc.psum_pool(name="product_banks", bufs=8 - FLIP_BANKS))
         stack.enter_context(tc.manual_schedule())
@@ -157,18 +158,24 @@ def tile_enhancedmathematicalreasoning_pa_t_kernel(tc, hidden_states, op_logits,
                 flip_pair(a)
             if a + 1 < PAIRS:
                 sort_pair(a + 1)
+            if a < PAIRS:
+                bias_terms(a * PAIR, PAIR)
 
         def flip_round(i):
             for n in range(PAIRS_PER_ROUND):
                 flip_pair(i * PAIRS_PER_ROUND + n)
 
-        def quantise_pair(a):
-            tiles = slice(a * PAIR, (a + 1) * PAIR)
+        def quantise_tiles(first, count):
+            in_pair = first % PAIR
+            tiles = slice(first, first + count)
             nc.vector.quantize_mx(
                 out=x_codes[:, tiles, :, :].rearrange("p j c t -> p (j c t)").bitcast(FP8X4),
                 scales=x_scales[:, tiles, :, :].rearrange("p j c t -> p (j c t)"),
-                in_=x_grouped[a][:].rearrange("p j c t v -> p (j c t v)"),
+                in_=x_grouped[first // PAIR][:, in_pair : in_pair + count, :, :, :].rearrange("p j c t v -> p (j c t v)"),
             )
+
+        def quantise_pair(a):
+            quantise_tiles(a * PAIR, PAIR)
 
         def quantise_round(i):
             for n in range(PAIRS_PER_ROUND):
@@ -236,30 +243,30 @@ def tile_enhancedmathematicalreasoning_pa_t_kernel(tc, hidden_states, op_logits,
         flip_pair(1)
         quantise_pair(0)
         regroup_weights(nc.vector.tensor_copy, 1, 0)
-        quantise_pair(1)
+        quantise_tiles(2, 1)
+        quantise_tiles(3, 1)
         regroup_weights(nc.vector.tensor_copy, 1, 1)
         quantise_weights(1)
 
         acc = keep.tile([P, TILES, HO], F32)
 
-        def bias_terms(i):
-            first = i * BIAS_TILES
+        def bias_terms(first, count):
             in_block = first % BIAS_BLOCK
-            bias_bank = banks.tile([P, BIAS_TILES, HO], F32, tag="bank")
+            bias_bank = banks.tile([P, count, HO], F32, tag="bank")
             nc.tensor.matmul(
                 out=bias_bank[:].rearrange("p j o -> p (j o)"),
                 lhsT=w_rows[:, first // BIAS_BLOCK, :],
-                rhs=be_diag[:, in_block : in_block + BIAS_TILES, :].rearrange("p j o -> p (j o)"),
+                rhs=be_diag[:, in_block : in_block + count, :].rearrange("p j o -> p (j o)"),
                 start=True,
                 stop=True,
             )
-            for n in range(BIAS_TILES):
+            for n in range(count):
                 j = first + n
                 nc.scalar.activation(
                     out=acc[:, j, :], in_=bias_bank[:, n, :], func=ACT.Copy, scale=inverse[:, j : j + 1]
                 )
 
-        def multiply_unit(i, g, spare=False):
+        def multiply(i, g, spare=False):
             products = []
             for b in range(ROUND_TILES // BANK_TILES):
                 if spare:
@@ -279,9 +286,31 @@ def tile_enhancedmathematicalreasoning_pa_t_kernel(tc, hidden_states, op_logits,
                             stop=(c == PASSES - 1),
                         )
                 products.append(product)
+            return products
+
+        def add_up(i, g, products):
+            shared = i == ROUNDS - 2 and g >= 2
+            if shared:
+                weighted = tail.tile([P, GROUP_EXPERTS, BANK_TILES, HO], F32, name="weighted")
+                for e in range(GROUP_EXPERTS):
+                    expert = g * GROUP_EXPERTS + e
+                    for n in range(BANK_TILES):
+                        j = i * ROUND_TILES + n
+                        nc.scalar.activation(
+                            out=weighted[:, e, n, :],
+                            in_=products[0][:, n, e, :],
+                            func=ACT.Copy,
+                            scale=op_w[:, j, expert : expert + 1],
+                        )
+                pair_sum = tail.tile([P, BANK_TILES, HO], F32, name="pair_sum")
+                nc.gpsimd.tensor_tensor(out=pair_sum[:], in0=weighted[:, 0, :, :], in1=weighted[:, 1, :, :], op=ALU.add)
+                if i in side:
+                    nc.gpsimd.tensor_tensor(out=side[i][:], in0=side[i][:], in1=pair_sum[:], op=ALU.add)
+                else:
+                    side[i] = pair_sum
             for e in range(GROUP_EXPERTS):
                 expert = g * GROUP_EXPERTS + e
-                for n in range(ROUND_TILES):
+                for n in range(BANK_TILES if shared else 0, ROUND_TILES):
                     j = i * ROUND_TILES + n
                     nc.vector.scalar_tensor_tensor(
                         out=acc[:, j, :],
@@ -292,22 +321,41 @@ def tile_enhancedmathematicalreasoning_pa_t_kernel(tc, hidden_states, op_logits,
                         op1=ALU.add,
                     )
 
-        bias_terms(0)
+        side = {}
+
+        def finish_round(i):
+            first = i * ROUND_TILES
+            if i in side:
+                shared = slice(first, first + BANK_TILES)
+                nc.gpsimd.tensor_tensor(out=side[i][:], in0=side[i][:], in1=acc[:, shared, :], op=ALU.add)
+                nc.sync.dma_start(out=out_dram[:, shared, :], in_=side[i][:])
+                first += BANK_TILES
+            last = (i + 1) * ROUND_TILES
+            step = last - first if i < ROUNDS - 1 else 1
+            for j in range(first, last, step):
+                nc.sync.dma_start(out=out_dram[:, j : j + step, :], in_=acc[:, j : j + step, :])
+
+        def multiply_unit(i, g, spare=False):
+            add_up(i, g, multiply(i, g, spare))
+
+        bias_terms(0, ROUND_TILES)
         for j in range(BIAS_TILES, BIAS_BLOCK):
             place_be(j)
         regroup_weights(nc.scalar.copy, 2, 0)
         multiply_unit(0, 0)
         regroup_weights(nc.vector.tensor_copy, 2, 1)
-        bias_terms(1)
+        bias_terms(1 * ROUND_TILES, ROUND_TILES)
         flip_pair(2)
-        multiply_unit(0, 1)
-        regroup_weights(nc.scalar.copy, 3, 0)
-        quantise_weights(2)
         flip_pair(3)
+        products = multiply(0, 1)
+        quantise_pair(2)
+        quantise_pair(3)
+        add_up(0, 1, products)
+        regroup_weights(nc.scalar.copy, 3, 0)
         regroup_weights(nc.scalar.copy, 3, 1)
-        quantise_round(1)
-        bias_terms(2)
+        quantise_weights(2)
         flip_pair(4)
+        bias_terms(2 * ROUND_TILES, PAIR)
         for s in range(1, ROUNDS + 1):
             units = [(s, 0), (s - 1, 2), (s, 1), (s - 1, 3)] if s < ROUNDS else [(s - 1, 2), (s - 1, 3)]
             for n, (i, g) in enumerate(units):
@@ -318,12 +366,8 @@ def tile_enhancedmathematicalreasoning_pa_t_kernel(tc, hidden_states, op_logits,
                     flip_next(2 * s + 3)
                 if n == 2:
                     flip_next(2 * s + 4)
-                if n == 2 and s + 2 < ROUNDS:
-                    bias_terms(s + 2)
                 if n == 0 and s + 1 < ROUNDS:
                     quantise_pair(PAIRS_PER_ROUND * (s + 1))
                 if n == 2 and s + 1 < ROUNDS:
                     quantise_pair(PAIRS_PER_ROUND * (s + 1) + 1)
-            step = ROUND_TILES if s < ROUNDS else 1
-            for j in range((s - 1) * ROUND_TILES, s * ROUND_TILES, step):
-                nc.sync.dma_start(out=out_dram[:, j : j + step, :], in_=acc[:, j : j + step, :])
+            finish_round(s - 1)

@@ -158,8 +158,6 @@ def tile_enhancedmathematicalreasoning_pa_t_kernel(tc, hidden_states, op_logits,
                 flip_pair(a)
             if a + 1 < PAIRS:
                 sort_pair(a + 1)
-            if a < PAIRS:
-                bias_terms(a * PAIR, PAIR)
 
         def flip_round(i):
             for n in range(PAIRS_PER_ROUND):
@@ -355,7 +353,7 @@ def tile_enhancedmathematicalreasoning_pa_t_kernel(tc, hidden_states, op_logits,
         regroup_weights(nc.scalar.copy, 3, 1)
         quantise_weights(2)
         flip_pair(4)
-        bias_terms(2 * ROUND_TILES, PAIR)
+        bias_terms(2 * ROUND_TILES, ROUND_TILES)
         for s in range(1, ROUNDS + 1):
             units = [(s, 0), (s - 1, 2), (s, 1), (s - 1, 3)] if s < ROUNDS else [(s - 1, 2), (s - 1, 3)]
             for n, (i, g) in enumerate(units):
@@ -366,6 +364,8 @@ def tile_enhancedmathematicalreasoning_pa_t_kernel(tc, hidden_states, op_logits,
                     flip_next(2 * s + 3)
                 if n == 2:
                     flip_next(2 * s + 4)
+                if n == 2 and s + 2 < ROUNDS:
+                    bias_terms((s + 2) * ROUND_TILES, ROUND_TILES)
                 if n == 0 and s + 1 < ROUNDS:
                     quantise_pair(PAIRS_PER_ROUND * (s + 1))
                 if n == 2 and s + 1 < ROUNDS:

from contextlib import ExitStack

import concourse.mybir as mybir
from concourse.masks import make_identity

F32 = mybir.dt.float32
BF16 = mybir.dt.bfloat16
U32 = mybir.dt.uint32
U8 = mybir.dt.uint8
FP8X4 = mybir.dt.float8_e4m3fn_x4
ALU = mybir.AluOpType
ACT = mybir.ActivationFunctionType
AXIS = mybir.AxisListType

P = 128
TOKENS = 4 * 1024
K = 1024
EXPERTS = 8
HO = 128
PACK = 4
PASSES = K // (P * PACK)
WORD_BLOCKS = K // 2 // P
TILES = TOKENS // P
BANK_F32 = 512
GROUP_EXPERTS = 2
GROUPS = EXPERTS // GROUP_EXPERTS
N_GROUP = GROUP_EXPERTS * HO
BANK_TILES = BANK_F32 // N_GROUP
PAIR = 2
PAIRS = TILES // PAIR
ROUND_TILES = 4
PAIRS_PER_ROUND = ROUND_TILES // PAIR
ROUNDS = TILES // ROUND_TILES
FLIP_BANKS = 4
RUN = 4
SPLIT = 2
BIAS_ROWS = SPLIT * EXPERTS
BIAS_BLOCK = P // BIAS_ROWS
BIAS_TILES = BANK_F32 // HO
assert BIAS_TILES == ROUND_TILES

FLOPS = 2 * TOKENS * K * EXPERTS * HO


def tile_enhancedmathematicalreasoning_pa_t_kernel(tc, hidden_states, op_logits, We, be, out):
    nc = tc.nc
    x_dram = hidden_states.flatten_outer_dims().rearrange("(p j) k -> p j k", j=TILES)
    logit_dram = op_logits.flatten_outer_dims().rearrange("(p j) e -> p j e", j=TILES)
    out_dram = out.flatten_outer_dims().rearrange("(p j) o -> p j o", j=TILES)

    with ExitStack() as stack:
        keep = stack.enter_context(tc.tile_pool(name="keep", bufs=1))
        stage = stack.enter_context(tc.tile_pool(name="stage", bufs=8))
        tail = stack.enter_context(tc.tile_pool(name="tail", bufs=2))
        banks = stack.enter_context(tc.psum_pool(name="banks", bufs=FLIP_BANKS))
        product_banks = stack.enter_context(tc.psum_pool(name="product_banks", bufs=8 - FLIP_BANKS))
        stack.enter_context(tc.manual_schedule())

        zeros = keep.tile([P, BANK_F32], BF16)
        nc.vector.memset(zeros[:], 0.0)

        def warm_up(count):
            idle = product_banks.tile([P, BANK_F32], F32, tag="product")
            for n in range(count):
                nc.tensor.matmul(out=idle[:], lhsT=zeros[:, 0:P], rhs=zeros[:], start=True, stop=True)

        warm_up(8)
        ident_bf = keep.tile([P, P], BF16)
        make_identity(nc, ident_bf[:])
        ident_f32 = keep.tile([P, P], F32)
        make_identity(nc, ident_f32[:])

        logit_bf = keep.tile([P, TILES, EXPERTS], BF16)
        nc.sync.dma_start(out=logit_bf[:], in_=logit_dram)

        w_raw = keep.tile([P, GROUPS, PASSES, GROUP_EXPERTS, PACK, HO], BF16)

        def load_weights(g, *passes):
            for c in passes or range(PASSES):
                first_row = c * PACK * P
                nc.sync.dma_start(
                    out=w_raw[:, g, c, :, :, :],
                    in_=We[
                        g * GROUP_EXPERTS : (g + 1) * GROUP_EXPERTS, first_row : first_row + PACK * P, :
                    ].rearrange("e (p v) o -> p e v o", v=PACK),
                )

        x_all = keep.tile([P, TILES, K], BF16)

        def load_tokens(first, count):
            tiles = slice(first, first + count)
            nc.sync.dma_start(out=x_all[:, tiles, :], in_=x_dram[:, tiles, :])

        be_rows = keep.tile([P, HO], BF16)
        nc.gpsimd.memset(be_rows[:], 0.0)
        nc.sync.dma_start(out=be_rows[0:EXPERTS, :], in_=be)
        for c in range(PASSES):
            load_tokens(c, 1)
            load_weights(0, c)
        for j in range(PASSES, ROUND_TILES):
            load_tokens(j, 1)
        load_weights(1)
        load_weights(2)
        for a in range(PAIRS_PER_ROUND, PAIRS):
            load_tokens(a * PAIR, PAIR)
            if a == 2 * PAIRS_PER_ROUND - 1:
                load_weights(3)

        w_grouped = keep.tile([P, GROUPS, PASSES, N_GROUP, PACK], BF16, align_bytes=64)
        w_codes = keep.tile([P, GROUPS, PASSES, N_GROUP], U32, align_bytes=64)
        w_scales = keep.tile([P, GROUPS, PASSES, N_GROUP], U8, align_bytes=64)

        def regroup_weights(copy, g, c):
            copy(
                out=w_grouped[:, g, c, :, :].rearrange("p (e q i) v -> p e q v i", e=GROUP_EXPERTS, i=RUN),
                in_=w_raw[:, g, c, :, :, :].rearrange("p e v (q i) -> p e q v i", i=RUN),
            )

        def quantise_weights(g):
            nc.vector.quantize_mx(
                out=w_codes[:, g, :, :].rearrange("p c n -> p (c n)").bitcast(FP8X4),
                scales=w_scales[:, g, :, :].rearrange("p c n -> p (c n)"),
                in_=w_grouped[:, g, :, :, :].rearrange("p c n v -> p (c n v)"),
            )

        x_codes = keep.tile([P, TILES, PASSES, P], U32, align_bytes=64)
        x_scales = keep.tile([P, TILES, PASSES, P], U8, align_bytes=64)
        x_grouped = {}
        x_sorted = {}

        def sort_pair(a):
            for j in range(a * PAIR, (a + 1) * PAIR):
                x_sorted[j] = stage.tile([P, PASSES, 2, P], F32, name="x_sorted")
                nc.scalar.copy(
                    out=x_sorted[j][:], in_=x_all[:, j, :].bitcast(F32).rearrange("p (c q u) -> p c u q", c=PASSES, u=2)
                )

        def flip_pair(a):
            x_grouped[a] = stage.tile([P, PAIR, PASSES, P, PACK], BF16, align_bytes=64, name="x_grouped")
            for jj in range(PAIR):
                j = a * PAIR + jj
                x_words = x_all[:, j, :].bitcast(F32)
                flipped = banks.tile([P, WORD_BLOCKS, P], F32, tag="bank")
                for c in range(PASSES):
                    for u in range(2):
                        nc.tensor.transpose(
                            flipped[:, 2 * c + u, :],
                            x_sorted[j][:, c, u, :] if j in x_sorted else x_words[:, 2 * c * P + u : 2 * (c + 1) * P : 2],
                            ident_f32[:],
                        )
                nc.scalar.copy(
                    out=x_grouped[a][:, jj, :, :, :].bitcast(F32),
                    in_=flipped[:].rearrange("p (c u) t -> p c t u", u=2),
                )

        def flip_next(a):
            if a < PAIRS:
                flip_pair(a)
            if a + 1 < PAIRS:
                sort_pair(a + 1)

        def flip_round(i):
            for n in range(PAIRS_PER_ROUND):
                flip_pair(i * PAIRS_PER_ROUND + n)

        def quantise_tiles(first, count):
            in_pair = first % PAIR
            tiles = slice(first, first + count)
            nc.vector.quantize_mx(
                out=x_codes[:, tiles, :, :].rearrange("p j c t -> p (j c t)").bitcast(FP8X4),
                scales=x_scales[:, tiles, :, :].rearrange("p j c t -> p (j c t)"),
                in_=x_grouped[first // PAIR][:, in_pair : in_pair + count, :, :, :].rearrange("p j c t v -> p (j c t v)"),
            )

        def quantise_pair(a):
            quantise_tiles(a * PAIR, PAIR)

        def quantise_round(i):
            for n in range(PAIRS_PER_ROUND):
                quantise_pair(i * PAIRS_PER_ROUND + n)

        repeat = keep.tile([P, P // EXPERTS, EXPERTS], BF16)
        nc.vector.tensor_copy(
            out=repeat[:], in_=ident_bf[:, 0:EXPERTS].unsqueeze(1).to_broadcast([P, P // EXPERTS, EXPERTS])
        )
        own_tile = keep.tile([P, BIAS_BLOCK], F32)
        nc.vector.tensor_reduce(
            out=own_tile[:], in_=ident_f32[:].rearrange("p (j r) -> p j r", r=BIAS_ROWS), axis=AXIS.X, op=ALU.add
        )
        top = keep.tile([P, TILES], F32)
        nc.vector.tensor_reduce(out=top[:], in_=logit_bf[:], axis=AXIS.X, op=ALU.max)
        shifted = keep.tile([P, TILES, EXPERTS], F32)
        nc.vector.tensor_tensor(
            out=shifted[:],
            in0=logit_bf[:],
            in1=top[:].unsqueeze(2).to_broadcast([P, TILES, EXPERTS]),
            op=ALU.subtract,
        )
        grown = keep.tile([P, TILES, EXPERTS], F32)
        nc.scalar.activation(out=grown[:], in_=shifted[:], func=ACT.Exp)
        grown_split = keep.tile([P, TILES, SPLIT, EXPERTS], BF16)
        nc.scalar.copy(out=grown_split[:, :, 0, :], in_=grown[:])
        be_bank = banks.tile([P, HO], F32, tag="bank")
        nc.tensor.matmul(
            out=be_bank[:], lhsT=repeat[:].rearrange("p r e -> p (r e)"), rhs=be_rows[:], start=True, stop=True
        )
        be_diag = keep.tile([P, BIAS_BLOCK, HO], BF16)

        def place_be(j):
            nc.scalar.activation(out=be_diag[:, j, :], in_=be_bank[:], func=ACT.Copy, scale=own_tile[:, j : j + 1])

        for j in range(BIAS_TILES):
            place_be(j)
        flip_pair(0)
        regroup_weights(nc.vector.tensor_copy, 0, 0)
        nc.vector.tensor_tensor(
            out=grown_split[:, :, 1, :], in0=grown[:], in1=grown_split[:, :, 0, :], op=ALU.subtract
        )
        total = keep.tile([P, TILES], F32)
        nc.vector.tensor_reduce(out=total[:], in_=grown[:], axis=AXIS.X, op=ALU.add)
        regroup_weights(nc.vector.tensor_copy, 0, 1)
        inverse = keep.tile([P, TILES], F32)
        nc.vector.reciprocal(out=inverse[:], in_=total[:])
        quantise_weights(0)
        op_w = keep.tile([P, TILES, EXPERTS], F32)
        nc.vector.tensor_tensor(
            out=op_w[:],
            in0=grown[:],
            in1=inverse[:].unsqueeze(2).to_broadcast([P, TILES, EXPERTS]),
            op=ALU.mult,
        )
        w_rows_bank = banks.tile([P, TILES // BIAS_BLOCK, P], BF16, tag="bank")
        for q in range(TILES // BIAS_BLOCK):
            nc.tensor.transpose(
                w_rows_bank[:, q, :],
                grown_split[:, q * BIAS_BLOCK : (q + 1) * BIAS_BLOCK, :, :].rearrange("p j s e -> p (j s e)"),
                ident_bf[:],
            )
        w_rows = keep.tile([P, TILES // BIAS_BLOCK, P], BF16)
        nc.scalar.copy(out=w_rows[:], in_=w_rows_bank[:])
        flip_pair(1)
        quantise_pair(0)
        regroup_weights(nc.vector.tensor_copy, 1, 0)
        quantise_tiles(2, 1)
        quantise_tiles(3, 1)
        regroup_weights(nc.vector.tensor_copy, 1, 1)
        quantise_weights(1)

        acc = keep.tile([P, TILES, HO], F32)

        def bias_terms(first, count):
            in_block = first % BIAS_BLOCK
            bias_bank = banks.tile([P, count, HO], F32, tag="bank")
            nc.tensor.matmul(
                out=bias_bank[:].rearrange("p j o -> p (j o)"),
                lhsT=w_rows[:, first // BIAS_BLOCK, :],
                rhs=be_diag[:, in_block : in_block + count, :].rearrange("p j o -> p (j o)"),
                start=True,
                stop=True,
            )
            for n in range(count):
                j = first + n
                nc.scalar.activation(
                    out=acc[:, j, :], in_=bias_bank[:, n, :], func=ACT.Copy, scale=inverse[:, j : j + 1]
                )

        def multiply(i, g, spare=False):
            products = []
            for b in range(ROUND_TILES // BANK_TILES):
                if spare:
                    product = banks.tile([P, BANK_TILES, GROUP_EXPERTS, HO], F32, tag="bank")
                else:
                    product = product_banks.tile([P, BANK_TILES, GROUP_EXPERTS, HO], F32, tag="product")
                for jj in range(BANK_TILES):
                    j = i * ROUND_TILES + b * BANK_TILES + jj
                    for c in range(PASSES):
                        nc.tensor.matmul_mx(
                            out=product[:, jj, :, :].rearrange("p e o -> p (e o)"),
                            lhsT=x_codes[:, j, c, :].bitcast(FP8X4),
                            lhsT_scale=x_scales[:, j, c, :],
                            rhs=w_codes[:, g, c, :].bitcast(FP8X4),
                            rhs_scale=w_scales[:, g, c, :],
                            start=(c == 0),
                            stop=(c == PASSES - 1),
                        )
                products.append(product)
            return products

        def add_up(i, g, products):
            shared = i == ROUNDS - 2 and g >= 2
            if shared:
                weighted = tail.tile([P, GROUP_EXPERTS, BANK_TILES, HO], F32, name="weighted")
                for e in range(GROUP_EXPERTS):
                    expert = g * GROUP_EXPERTS + e
                    for n in range(BANK_TILES):
                        j = i * ROUND_TILES + n
                        nc.scalar.activation(
                            out=weighted[:, e, n, :],
                            in_=products[0][:, n, e, :],
                            func=ACT.Copy,
                            scale=op_w[:, j, expert : expert + 1],
                        )
                pair_sum = tail.tile([P, BANK_TILES, HO], F32, name="pair_sum")
                nc.gpsimd.tensor_tensor(out=pair_sum[:], in0=weighted[:, 0, :, :], in1=weighted[:, 1, :, :], op=ALU.add)
                if i in side:
                    nc.gpsimd.tensor_tensor(out=side[i][:], in0=side[i][:], in1=pair_sum[:], op=ALU.add)
                else:
                    side[i] = pair_sum
            for e in range(GROUP_EXPERTS):
                expert = g * GROUP_EXPERTS + e
                for n in range(BANK_TILES if shared else 0, ROUND_TILES):
                    j = i * ROUND_TILES + n
                    nc.vector.scalar_tensor_tensor(
                        out=acc[:, j, :],
                        in0=products[n // BANK_TILES][:, n % BANK_TILES, e, :],
                        scalar=op_w[:, j, expert : expert + 1],
                        in1=acc[:, j, :],
                        op0=ALU.mult,
                        op1=ALU.add,
                    )

        side = {}

        def finish_round(i):
            first = i * ROUND_TILES
            if i in side:
                shared = slice(first, first + BANK_TILES)
                nc.gpsimd.tensor_tensor(out=side[i][:], in0=side[i][:], in1=acc[:, shared, :], op=ALU.add)
                nc.sync.dma_start(out=out_dram[:, shared, :], in_=side[i][:])
                first += BANK_TILES
            last = (i + 1) * ROUND_TILES
            step = last - first if i < ROUNDS - 1 else 1
            for j in range(first, last, step):
                nc.sync.dma_start(out=out_dram[:, j : j + step, :], in_=acc[:, j : j + step, :])

        def multiply_unit(i, g, spare=False):
            add_up(i, g, multiply(i, g, spare))

        bias_terms(0, ROUND_TILES)
        for j in range(BIAS_TILES, BIAS_BLOCK):
            place_be(j)
        regroup_weights(nc.scalar.copy, 2, 0)
        multiply_unit(0, 0)
        regroup_weights(nc.vector.tensor_copy, 2, 1)
        bias_terms(1 * ROUND_TILES, ROUND_TILES)
        flip_pair(2)
        flip_pair(3)
        products = multiply(0, 1)
        quantise_pair(2)
        quantise_pair(3)
        add_up(0, 1, products)
        regroup_weights(nc.scalar.copy, 3, 0)
        regroup_weights(nc.scalar.copy, 3, 1)
        quantise_weights(2)
        flip_pair(4)
        bias_terms(2 * ROUND_TILES, ROUND_TILES)
        for s in range(1, ROUNDS + 1):
            units = [(s, 0), (s - 1, 2), (s, 1), (s - 1, 3)] if s < ROUNDS else [(s - 1, 2), (s - 1, 3)]
            for n, (i, g) in enumerate(units):
                multiply_unit(i, g, spare=s >= ROUNDS - 1 and n % 2 == 0)
                if n == 0 and s == 1:
                    quantise_weights(3)
                if n == 0:
                    flip_next(2 * s + 3)
                if n == 2:
                    flip_next(2 * s + 4)
                if n == 2 and s + 2 < ROUNDS:
                    bias_terms((s + 2) * ROUND_TILES, ROUND_TILES)
                if n == 0 and s + 1 < ROUNDS:
                    quantise_pair(PAIRS_PER_ROUND * (s + 1))
                if n == 2 and s + 1 < ROUNDS:
                    quantise_pair(PAIRS_PER_ROUND * (s + 1) + 1)
            finish_round(s - 1)
